import numpy as np
import ml_dtypes


def mxq(x, axis, fmt="e4m3"):
    dtype, down = {"e4m3": (ml_dtypes.float8_e4m3fn, 7), "e5m2": (ml_dtypes.float8_e5m2, 14)}[fmt]
    v = np.moveaxis(np.asarray(x, np.float32).astype(ml_dtypes.bfloat16).astype(np.float64), axis, -1)
    blocks = v.reshape(v.shape[:-1] + (-1, 32))
    amax = np.abs(blocks).max(-1, keepdims=True)
    byte = np.maximum(np.where(amax > 0, np.frexp(amax)[1] - 1 + 127, 0) - down, 1)
    scale = np.exp2(byte - 127.0)
    codes = (blocks / scale).astype(np.float32).astype(dtype).astype(np.float64)
    return np.moveaxis((codes * scale).reshape(v.shape), -1, axis)


WIDE = False


def mx_kscale(k):
    if not WIDE:
        return np.ones(k)
    levels = np.array([10, -10, 5, -5, 0])
    if k % 512:
        return np.exp2(np.random.permutation(np.resize(levels, k // 32))).repeat(32)
    a = np.empty((k // 512, 16))
    for p in range(k // 512):
        a[p, :8] = np.random.permutation(np.resize(levels, 8))
        for g in range(8):
            far = levels[np.abs(levels - a[p, g]) >= 10]
            a[p, g + 8] = far[np.random.randint(len(far))]
    return np.exp2(a.ravel()).repeat(32)


BF16 = ml_dtypes.bfloat16


def bf(x):
    return np.asarray(x, np.float32).astype(BF16)


def f64(x):
    return np.asarray(x).astype(np.float64)


B, K, N = 1024, 2048, 2048
EPS = 1e-5
GELU_C = 0.7978845608


def setup_inputs():
    s = mx_kscale(K)
    return {"x": bf(np.random.standard_normal((B, K)) * s),
            "weight": bf(np.random.standard_normal((K, N)) * np.sqrt(2.0 / K) / s[:, None]),
            "bn_gamma": bf(np.random.uniform(0.5, 1.5, N)),
            "bn_beta": bf(np.random.standard_normal(N) * 0.1),
            "bn_mean": bf(np.random.standard_normal(N) * 0.1),
            "bn_var": bf(np.random.uniform(0.5, 1.5, N))}


def core(x, weight, bn_gamma, bn_beta, bn_mean, bn_var):
    acc = mxq(f64(x), 1, "e4m3") @ mxq(f64(weight), 0, "e4m3")
    x_norm = (acc - f64(bn_mean)) / np.sqrt(f64(bn_var) + EPS)
    bn_out = f64(bn_gamma) * x_norm + f64(bn_beta)
    gelu = 0.5 * bn_out * (1.0 + np.tanh(GELU_C * (bn_out + 0.044715 * bn_out * bn_out * bn_out)))
    return np.maximum(gelu, 0.0)


def e4m3fn_bytes(y):
    return np.clip(np.asarray(y, np.float64), -448.0, 448.0).astype(np.float32).astype(ml_dtypes.float8_e4m3fn).view(np.uint8)


def reference(x, weight, bn_gamma, bn_beta, bn_mean, bn_var):
    out = core(x, weight, bn_gamma, bn_beta, bn_mean, bn_var)
    s = np.max(np.abs(out)) / 448.0
    return out, e4m3fn_bytes(out / s)

@@ -1,0 +1,295 @@
+from contextlib import ExitStack
+
+import concourse.mybir as mybir
+from concourse.masks import make_identity
+
+B, K, N = 1024, 2048, 2048
+EPS = 1e-5
+FLOPS = 2 * B * K * N
+
+F32 = mybir.dt.float32
+BF16 = mybir.dt.bfloat16
+U32 = mybir.dt.uint32
+U8 = mybir.dt.uint8
+FP8X4 = mybir.dt.float8_e4m3fn_x4
+FP8 = mybir.dt.float8_e4m3fn
+ACT = mybir.ActivationFunctionType
+ALU = mybir.AluOpType
+AX = mybir.AxisListType
+
+P = 128
+PASSES = 4
+CHUNKS = 4
+HALVES = 2
+CW = 512
+HW = 512
+VW = 288
+SW = 1024
+SV = 736
+
+
+def tile_modelnew_kernel(tc, x, weight, bn_gamma, bn_beta, bn_mean, bn_var, out_0, out_1):
+    nc = tc.nc
+    with ExitStack() as ctx:
+        consts = ctx.enter_context(tc.tile_pool(name="consts", bufs=1))
+        ld = ctx.enter_context(tc.tile_pool(name="ld", bufs=12))
+        gxp = ctx.enter_context(tc.tile_pool(name="gxp", bufs=4))
+        xq = ctx.enter_context(tc.tile_pool(name="xq", bufs=1))
+        wgp = ctx.enter_context(tc.tile_pool(name="wgp", bufs=3))
+        wq = ctx.enter_context(tc.tile_pool(name="wq", bufs=1))
+        gtp = ctx.enter_context(tc.tile_pool(name="gtp", bufs=8))
+        outp = ctx.enter_context(tc.tile_pool(name="outp", bufs=1))
+        f8p = ctx.enter_context(tc.tile_pool(name="f8p", bufs=8))
+        psum = ctx.enter_context(tc.psum_pool(name="psum", bufs=4))
+        ctx.enter_context(tc.manual_schedule(engines={mybir.EngineType.PE}))
+
+        ident = consts.tile([P, P], F32, name="ident")
+        make_identity(nc, ident[:])
+
+        bn_raw = consts.tile([P, P], BF16, name="bn_raw")
+        nc.vector.memset(bn_raw[64:128, :], 0.0)
+        for v, vec in enumerate((bn_gamma, bn_beta, bn_mean, bn_var)):
+            nc.sync.dma_start(out=bn_raw[16 * v:16 * v + 16, :], in_=vec.rearrange("(t p) -> t p", p=P))
+
+        one = consts.tile([P, 1], F32, name="one")
+        nc.vector.memset(one[:], 1.0)
+        warm = consts.tile([P, 1], F32, name="warm")
+        nc.scalar.activation(out=warm[:], in_=one[:], func=ACT.Sqrt)
+
+        x_sb = []
+        for m in range(8):
+            t = ld.tile([P, K], BF16, name="x%d" % m, tag="ld")
+            nc.sync.dma_start(out=t[:], in_=x[P * m:P * (m + 1), :])
+            x_sb.append(t)
+        w_raw = {}
+
+        def w_load(c):
+            for p in range(PASSES):
+                t = ld.tile([P, 4, CW], BF16, name="w%d_%d" % (c, p), tag="ld")
+                nc.sync.dma_start(
+                    out=t[:],
+                    in_=weight[512 * p:512 * (p + 1), CW * c:CW * (c + 1)].rearrange("(p j) w -> p j w", j=4),
+                )
+                w_raw[(c, p)] = t
+
+        w_load(0)
+
+        bn_f = consts.tile([P, P], F32, name="bn_f")
+        nc.vector.tensor_copy(out=bn_f[:], in_=bn_raw[:])
+        bn_ps = psum.tile([P, P], F32, name="bn_ps", tag="tp")
+        nc.tensor.transpose(out=bn_ps[:], in_=bn_f[:], identity=ident[:])
+        bnT = consts.tile([P, 64], F32, name="bnT")
+        nc.vector.tensor_copy(out=bnT[:], in_=bn_ps[:, 0:64])
+        ve = consts.tile([P, 16], F32, name="ve")
+        nc.vector.tensor_scalar(out=ve[:], in0=bnT[:, 48:64], scalar1=EPS, scalar2=None, op0=ALU.add)
+        sd = consts.tile([P, 16], F32, name="sd")
+        nc.scalar.activation(out=sd[:], in_=ve[:], func=ACT.Sqrt)
+        warm2 = consts.tile([P, 1], F32, name="warm2")
+        nc.scalar.activation(out=warm2[:], in_=sd[:, 0:1], func=ACT.Gelu_apprx_tanh)
+        rs = consts.tile([P, 16], F32, name="rs")
+        nc.vector.reciprocal(out=rs[:], in_=sd[:])
+        aa = consts.tile([P, 16], F32, name="aa")
+        nc.vector.tensor_tensor(out=aa[:], in0=bnT[:, 0:16], in1=rs[:], op=ALU.mult)
+        ma = consts.tile([P, 16], F32, name="ma")
+        nc.vector.tensor_tensor(out=ma[:], in0=bnT[:, 32:48], in1=aa[:], op=ALU.mult)
+        cc = consts.tile([P, 16], F32, name="cc")
+        nc.vector.tensor_tensor(out=cc[:], in0=bnT[:, 16:32], in1=ma[:], op=ALU.subtract)
+
+        xc = {}
+        xs = {}
+        for g in range(PASSES):
+            for h in range(HALVES):
+                xc[(g, h)] = xq.tile([P, HW], U32, name="xc%d_%d" % (g, h), align_bytes=64)
+                xs[(g, h)] = xq.tile([P, HW], U8, name="xs%d_%d" % (g, h), align_bytes=64)
+        xt_ps = {}
+
+        def x_turn(q, g):
+            xt = psum.tile([P, 2, 256], F32, name="xt", tag="tp")
+            for mi in range(2):
+                words = x_sb[2 * q + mi][:].bitcast(F32)
+                for u in range(2):
+                    nc.tensor.transpose(
+                        out=xt[:, u, P * mi:P * (mi + 1)],
+                        in_=words[:, 256 * g + u:256 * (g + 1):2],
+                        identity=ident[:],
+                    )
+            xt_ps[(q, g)] = xt
+
+        def x_quant(q, g):
+            h = q // 2
+            cols = slice(256 * (q % 2), 256 * (q % 2) + 256)
+            gx = gxp.tile([P, 1024], BF16, name="gx", tag="gx", align_bytes=64)
+            dst = gx[:].bitcast(F32).rearrange("p (r u) -> p r u", u=2)
+            src = xt_ps[(q, g)][:].rearrange("p u r -> p r u")
+            on_scalar = (g >= 2) if q == 0 else (g < 3)
+            if on_scalar:
+                nc.scalar.copy(out=dst, in_=src)
+            else:
+                nc.vector.tensor_copy(out=dst, in_=src)
+            nc.vector.quantize_mx(out=xc[(g, h)][:, cols].bitcast(FP8X4), scales=xs[(g, h)][:, cols], in_=gx[:])
+
+        wc = {}
+        ws = {}
+        wg_sb = {}
+
+        def w_weave(c, p):
+            wr = w_raw[(c, p)]
+            wg = wgp.tile([P, CW, 4], BF16, name="wg", tag="wg", align_bytes=64)
+            nc.vector.tensor_copy(out=wg[:, 0:VW, :], in_=wr[:, :, 0:VW].rearrange("p j w -> p w j"))
+            nc.scalar.copy(out=wg[:, VW:CW, :], in_=wr[:, :, VW:CW].rearrange("p j w -> p w j"))
+            wg_sb[(c, p)] = wg
+
+        def w_quant(c, p):
+            wc[(c, p)] = wq.tile([P, CW], U32, name="wc%d_%d" % (c, p), align_bytes=64)
+            ws[(c, p)] = wq.tile([P, CW], U8, name="ws%d_%d" % (c, p), align_bytes=64)
+            nc.vector.quantize_mx(
+                out=wc[(c, p)][:].bitcast(FP8X4), scales=ws[(c, p)][:],
+                in_=wg_sb[(c, p)][:].rearrange("p w j -> p (w j)"),
+            )
+
+        for q in range(3):
+            for g in range(PASSES):
+                x_turn(q, g)
+                x_quant(q, g)
+            if q == 1:
+                w_load(1)
+        for g in range(PASSES):
+            x_turn(3, g)
+        w_load(2)
+        w_weave(0, 0)
+        w_quant(0, 0)
+        x_quant(3, 0)
+        x_quant(3, 1)
+        w_weave(0, 1)
+        w_quant(0, 1)
+        x_quant(3, 2)
+        x_quant(3, 3)
+        w_weave(0, 2)
+        w_quant(0, 2)
+        w_weave(0, 3)
+        w_quant(0, 3)
+        w_load(3)
+
+        stat = consts.tile([P, 32], F32, name="stat")
+        o_sb = []
+        for m in range(8):
+            o = outp.tile([P, N], F32, name="o%d" % m)
+            o_sb.append(o)
+        g_sb = {}
+
+        def mx(acc, c, h, j, p):
+            nc.tensor.matmul_mx(
+                out=acc[:],
+                lhsT=wc[(c, p)][:, P * j:P * (j + 1)].bitcast(FP8X4),
+                lhsT_scale=ws[(c, p)][:, P * j:P * (j + 1)],
+                rhs=xc[(p, h)][:].bitcast(FP8X4),
+                rhs_scale=xs[(p, h)][:],
+                start=(p == 0),
+                stop=(p == PASSES - 1),
+            )
+
+        def gelu(acc, c, h, j):
+            nt = 4 * c + j
+            gt = gtp.tile([P, HW], F32, name="gt", tag="gt")
+            nc.scalar.activation(
+                out=gt[:], in_=acc[:], func=ACT.Gelu_apprx_tanh, bias=cc[:, nt:nt + 1], scale=aa[:, nt:nt + 1]
+            )
+            g_sb[(c, h, j)] = gt
+
+        def back(c, h):
+            for mi in range(4):
+                m = 4 * h + mi
+                tp = psum.tile([P, CW], F32, name="tp", tag="tp")
+                for j in range(4):
+                    nc.tensor.transpose(
+                        out=tp[:, P * j:P * (j + 1)], in_=g_sb[(c, h, j)][:, P * mi:P * (mi + 1)], identity=ident[:]
+                    )
+                k = 8 * c + m
+                nc.vector.tensor_scalar(
+                    out=o_sb[m][:, CW * c:CW * (c + 1)], in0=tp[:], scalar1=0.0, scalar2=None,
+                    op0=ALU.max, op1=ALU.max, accum_out=stat[:, k:k + 1],
+                )
+                nc.sync.dma_start(out=out_0[P * m:P * (m + 1), CW * c:CW * (c + 1)], in_=o_sb[m][:, CW * c:CW * (c + 1)])
+
+        plan = {0: ((1, 0), (1, 1)), 1: ((1, 2), (1, 3)), 2: ((2, 0), (2, 1)), 3: ((2, 2), (2, 3)),
+                4: ((3, 0), (3, 1)), 5: ((3, 2), (3, 3))}
+        units = [(c, h) for c in range(CHUNKS) for h in range(HALVES)]
+        last = len(units) - 1
+        for ui, (c, h) in enumerate(units):
+            todo = plan.get(ui, ())
+            if ui == 0:
+                accs = []
+                for j in range(4):
+                    acc = psum.tile([P, HW], F32, name="acc", tag="acc")
+                    accs.append(acc)
+                for p in range(PASSES):
+                    for j in range(4):
+                        mx(accs[j], c, h, j, p)
+                w_weave(1, 0)
+                gelu(accs[0], c, h, 0)
+                gelu(accs[1], c, h, 1)
+                w_weave(1, 1)
+                w_quant(1, 0)
+                gelu(accs[2], c, h, 2)
+                gelu(accs[3], c, h, 3)
+                w_quant(1, 1)
+                continue
+            after = 2 if ui == 1 else 1
+            for j in range(4):
+                acc = psum.tile([P, HW], F32, name="acc", tag="acc")
+                for p in range(PASSES):
+                    mx(acc, c, h, j, p)
+                if j == 0 and todo:
+                    w_weave(todo[0][0], todo[0][1])
+                gelu(acc, c, h, j)
+                if ui == last:
+                    k = 8 * c + 4 * h + j
+                    nc.vector.tensor_reduce(out=stat[:, k:k + 1], in_=g_sb[(c, h, j)][:], axis=AX.X, op=ALU.max)
+                if j == 1 and todo:
+                    w_quant(todo[0][0], todo[0][1])
+                    w_weave(todo[1][0], todo[1][1])
+                if j == after:
+                    back(units[ui - 1][0], units[ui - 1][1])
+                if j == 2 and todo:
+                    w_quant(todo[1][0], todo[1][1])
+
+        c, h = units[last]
+        tps = []
+        for mi in range(4):
+            tp = psum.tile([P, CW], F32, name="tp", tag="tp")
+            tps.append(tp)
+        for j in range(4):
+            for mi in range(4):
+                nc.tensor.transpose(
+                    out=tps[mi][:, P * j:P * (j + 1)], in_=g_sb[(c, h, j)][:, P * mi:P * (mi + 1)], identity=ident[:]
+                )
+
+        junk = consts.tile([P, 32], F32, name="junk")
+        part = consts.tile([P, 1], F32, name="part")
+        nc.vector.tensor_scalar(
+            out=junk[:], in0=stat[:], scalar1=1.0 / 448.0, scalar2=None, op0=ALU.mult, op1=ALU.max, accum_out=part[:]
+        )
+        pt = psum.tile([P, P], F32, name="pt", tag="acc")
+        nc.tensor.transpose(out=pt[:], in_=part[:, 0:1].to_broadcast([P, P]), identity=ident[:])
+        s_all = consts.tile([P, 1], F32, name="s_all")
+        nc.vector.tensor_reduce(out=s_all[:], in_=pt[:], axis=AX.X, op=ALU.max)
+        inv = consts.tile([P, 1], F32, name="inv")
+        nc.vector.reciprocal(out=inv[:], in_=s_all[:])
+
+        for mi in range(4):
+            m = 4 * h + mi
+            nc.scalar.activation(out=o_sb[m][:, CW * c:CW * (c + 1)], in_=tps[mi][:], func=ACT.Relu)
+            nc.sync.dma_start(out=out_0[P * m:P * (m + 1), CW * c:CW * (c + 1)], in_=o_sb[m][:, CW * c:CW * (c + 1)])
+
+        for m in range(8):
+            f8 = f8p.tile([P, N], FP8, name="f8", tag="f8")
+            for s in range(N // SW):
+                tmp = ld.tile([P, SW], F32, name="tmp", tag="ld")
+                lo = SW * s
+                nc.vector.tensor_scalar(
+                    out=tmp[:, 0:SV], in0=o_sb[m][:, lo:lo + SV], scalar1=inv[:, 0:1], scalar2=None, op0=ALU.mult
+                )
+                nc.scalar.activation(out=tmp[:, SV:SW], in_=o_sb[m][:, lo + SV:lo + SW], func=ACT.Copy, scale=inv[:, 0:1])
+                nc.vector.tensor_copy(out=f8[:, lo:lo + SV], in_=tmp[:, 0:SV], saturate=False)
+                nc.scalar.copy(out=f8[:, lo + SV:lo + SW], in_=tmp[:, SV:SW], saturate=False)
+            nc.sync.dma_start(out=out_1[P * m:P * (m + 1), :], in_=f8[:].bitcast(U8))

@@ -25,6 +25,7 @@ CW = 512
 HW = 512
 VW = 288
 SW = 1024
+WARM_UP = 8
 SV = 736
 
 
@@ -45,6 +46,18 @@ def tile_modelnew_kernel(tc, x, weight, bn_gamma, bn_beta, bn_mean, bn_var, out_
 
         ident = consts.tile([P, P], F32, name="ident")
         make_identity(nc, ident[:])
+
+        zw = consts.tile([P, P], BF16, name="zw")
+        nc.vector.memset(zw[:], 0.0)
+        zx = consts.tile([P, 512], BF16, name="zx")
+        nc.vector.memset(zx[:], 0.0)
+        idle_ps = psum.tile([P, 512], F32, name="idle_ps", tag="acc")
+
+        def keep_warm(n):
+            for i in range(n):
+                nc.tensor.matmul(out=idle_ps[:], lhsT=zw[:], rhs=zx[:], start=True, stop=True)
+
+        keep_warm(WARM_UP)
 
         bn_raw = consts.tile([P, P], BF16, name="bn_raw")
         nc.vector.memset(bn_raw[64:128, :], 0.0)
@@ -113,6 +126,7 @@ def tile_modelnew_kernel(tc, x, weight, bn_gamma, bn_beta, bn_mean, bn_var, out_
                         in_=words[:, 256 * g + u:256 * (g + 1):2],
                         identity=ident[:],
                     )
+            keep_warm(1)
             xt_ps[(q, g)] = xt
 
         def x_quant(q, g):
@@ -121,11 +135,7 @@ def tile_modelnew_kernel(tc, x, weight, bn_gamma, bn_beta, bn_mean, bn_var, out_
             gx = gxp.tile([P, 1024], BF16, name="gx", tag="gx", align_bytes=64)
             dst = gx[:].bitcast(F32).rearrange("p (r u) -> p r u", u=2)
             src = xt_ps[(q, g)][:].rearrange("p u r -> p r u")
-            on_scalar = (g >= 2) if q == 0 else (g < 3)
-            if on_scalar:
-                nc.scalar.copy(out=dst, in_=src)
-            else:
-                nc.vector.tensor_copy(out=dst, in_=src)
+            nc.scalar.copy(out=dst, in_=src)
             nc.vector.quantize_mx(out=xc[(g, h)][:, cols].bitcast(FP8X4), scales=xs[(g, h)][:, cols], in_=gx[:])
 
         wc = {}
@@ -147,7 +157,23 @@ def tile_modelnew_kernel(tc, x, weight, bn_gamma, bn_beta, bn_mean, bn_var, out_
                 in_=wg_sb[(c, p)][:].rearrange("p w j -> p (w j)"),
             )
 
-        for q in range(3):
+        for g in range(PASSES):
+            xt = psum.tile([P, 2, 256], F32, name="xt", tag="tp")
+            xt_ps[(0, g)] = xt
+        for mi in range(2):
+            words = x_sb[mi][:].bitcast(F32)
+            for g in range(PASSES):
+                for u in range(2):
+                    nc.tensor.transpose(
+                        out=xt_ps[(0, g)][:, u, P * mi:P * (mi + 1)],
+                        in_=words[:, 256 * g + u:256 * (g + 1):2],
+                        identity=ident[:],
+                    )
+                if g % 2 == 1:
+                    keep_warm(1)
+        for g in range(PASSES):
+            x_quant(0, g)
+        for q in range(1, 3):
             for g in range(PASSES):
                 x_turn(q, g)
                 x_quant(q, g)
@@ -281,15 +307,33 @@ def tile_modelnew_kernel(tc, x, weight, bn_gamma, bn_beta, bn_mean, bn_var, out_
             nc.scalar.activation(out=o_sb[m][:, CW * c:CW * (c + 1)], in_=tps[mi][:], func=ACT.Relu)
             nc.sync.dma_start(out=out_0[P * m:P * (m + 1), CW * c:CW * (c + 1)], in_=o_sb[m][:, CW * c:CW * (c + 1)])
 
-        for m in range(8):
-            f8 = f8p.tile([P, N], FP8, name="f8", tag="f8")
-            for s in range(N // SW):
-                tmp = ld.tile([P, SW], F32, name="tmp", tag="ld")
-                lo = SW * s
-                nc.vector.tensor_scalar(
-                    out=tmp[:, 0:SV], in0=o_sb[m][:, lo:lo + SV], scalar1=inv[:, 0:1], scalar2=None, op0=ALU.mult
-                )
-                nc.scalar.activation(out=tmp[:, SV:SW], in_=o_sb[m][:, lo + SV:lo + SW], func=ACT.Copy, scale=inv[:, 0:1])
-                nc.vector.tensor_copy(out=f8[:, lo:lo + SV], in_=tmp[:, 0:SV], saturate=False)
-                nc.scalar.copy(out=f8[:, lo + SV:lo + SW], in_=tmp[:, SV:SW], saturate=False)
-            nc.sync.dma_start(out=out_1[P * m:P * (m + 1), :], in_=f8[:].bitcast(U8))
+        steps = [(m, s) for m in range(8) for s in range(N // SW)]
+        f8_sb = {}
+        tmp_sb = {}
+
+        def scale(m, s):
+            tmp = ld.tile([P, SW], F32, name="tmp", tag="ld")
+            lo = SW * s
+            nc.vector.tensor_scalar(
+                out=tmp[:, 0:SV], in0=o_sb[m][:, lo:lo + SV], scalar1=inv[:, 0:1], scalar2=None, op0=ALU.mult
+            )
+            nc.scalar.activation(out=tmp[:, SV:SW], in_=o_sb[m][:, lo + SV:lo + SW], func=ACT.Copy, scale=inv[:, 0:1])
+            tmp_sb[(m, s)] = tmp
+
+        def cast(m, s):
+            if s == 0:
+                f8 = f8p.tile([P, N], FP8, name="f8", tag="f8")
+                f8_sb[m] = f8
+            f8 = f8_sb[m]
+            tmp = tmp_sb[(m, s)]
+            lo = SW * s
+            nc.vector.tensor_copy(out=f8[:, lo:lo + SV], in_=tmp[:, 0:SV], saturate=False)
+            nc.scalar.copy(out=f8[:, lo + SV:lo + SW], in_=tmp[:, SV:SW], saturate=False)
+            if s == N // SW - 1:
+                nc.sync.dma_start(out=out_1[P * m:P * (m + 1), :], in_=f8[:].bitcast(U8))
+
+        scale(steps[0][0], steps[0][1])
+        for i in range(1, len(steps)):
+            scale(steps[i][0], steps[i][1])
+            cast(steps[i - 1][0], steps[i - 1][1])
+        cast(steps[-1][0], steps[-1][1])

@@ -25,7 +25,6 @@ CW = 512
 HW = 512
 VW = 288
 SW = 1024
-WARM_UP = 8
 SV = 736
 
 
@@ -46,18 +45,6 @@ def tile_modelnew_kernel(tc, x, weight, bn_gamma, bn_beta, bn_mean, bn_var, out_
 
         ident = consts.tile([P, P], F32, name="ident")
         make_identity(nc, ident[:])
-
-        zw = consts.tile([P, P], BF16, name="zw")
-        nc.vector.memset(zw[:], 0.0)
-        zx = consts.tile([P, 512], BF16, name="zx")
-        nc.vector.memset(zx[:], 0.0)
-        idle_ps = psum.tile([P, 512], F32, name="idle_ps", tag="acc")
-
-        def keep_warm(n):
-            for i in range(n):
-                nc.tensor.matmul(out=idle_ps[:], lhsT=zw[:], rhs=zx[:], start=True, stop=True)
-
-        keep_warm(WARM_UP)
 
         bn_raw = consts.tile([P, P], BF16, name="bn_raw")
         nc.vector.memset(bn_raw[64:128, :], 0.0)
@@ -126,7 +113,6 @@ def tile_modelnew_kernel(tc, x, weight, bn_gamma, bn_beta, bn_mean, bn_var, out_
                         in_=words[:, 256 * g + u:256 * (g + 1):2],
                         identity=ident[:],
                     )
-            keep_warm(1)
             xt_ps[(q, g)] = xt
 
         def x_quant(q, g):
@@ -135,7 +121,11 @@ def tile_modelnew_kernel(tc, x, weight, bn_gamma, bn_beta, bn_mean, bn_var, out_
             gx = gxp.tile([P, 1024], BF16, name="gx", tag="gx", align_bytes=64)
             dst = gx[:].bitcast(F32).rearrange("p (r u) -> p r u", u=2)
             src = xt_ps[(q, g)][:].rearrange("p u r -> p r u")
-            nc.scalar.copy(out=dst, in_=src)
+            on_scalar = (g >= 2) if q == 0 else (g < 3)
+            if on_scalar:
+                nc.scalar.copy(out=dst, in_=src)
+            else:
+                nc.vector.tensor_copy(out=dst, in_=src)
             nc.vector.quantize_mx(out=xc[(g, h)][:, cols].bitcast(FP8X4), scales=xs[(g, h)][:, cols], in_=gx[:])
 
         wc = {}
@@ -145,8 +135,14 @@ def tile_modelnew_kernel(tc, x, weight, bn_gamma, bn_beta, bn_mean, bn_var, out_
         def w_weave(c, p):
             wr = w_raw[(c, p)]
             wg = wgp.tile([P, CW, 4], BF16, name="wg", tag="wg", align_bytes=64)
-            nc.vector.tensor_copy(out=wg[:, 0:VW, :], in_=wr[:, :, 0:VW].rearrange("p j w -> p w j"))
-            nc.scalar.copy(out=wg[:, VW:CW, :], in_=wr[:, :, VW:CW].rearrange("p j w -> p w j"))
+            nc.vector.tensor_copy(
+                out=wg[:, 0:VW, :].rearrange("p (c i) j -> p c j i", i=4),
+                in_=wr[:, :, 0:VW].rearrange("p j (c i) -> p c j i", i=4),
+            )
+            nc.scalar.copy(
+                out=wg[:, VW:CW, :].rearrange("p (c i) j -> p c j i", i=4),
+                in_=wr[:, :, VW:CW].rearrange("p j (c i) -> p c j i", i=4),
+            )
             wg_sb[(c, p)] = wg
 
         def w_quant(c, p):
@@ -157,23 +153,7 @@ def tile_modelnew_kernel(tc, x, weight, bn_gamma, bn_beta, bn_mean, bn_var, out_
                 in_=wg_sb[(c, p)][:].rearrange("p w j -> p (w j)"),
             )
 
-        for g in range(PASSES):
-            xt = psum.tile([P, 2, 256], F32, name="xt", tag="tp")
-            xt_ps[(0, g)] = xt
-        for mi in range(2):
-            words = x_sb[mi][:].bitcast(F32)
-            for g in range(PASSES):
-                for u in range(2):
-                    nc.tensor.transpose(
-                        out=xt_ps[(0, g)][:, u, P * mi:P * (mi + 1)],
-                        in_=words[:, 256 * g + u:256 * (g + 1):2],
-                        identity=ident[:],
-                    )
-                if g % 2 == 1:
-                    keep_warm(1)
-        for g in range(PASSES):
-            x_quant(0, g)
-        for q in range(1, 3):
+        for q in range(3):
             for g in range(PASSES):
                 x_turn(q, g)
                 x_quant(q, g)

@@ -25,7 +25,8 @@ CW = 512
 HW = 512
 VW = 288
 SW = 1024
-SV = 736
+SV = (1024, 608)
+LATE = 4
 
 
 def tile_modelnew_kernel(tc, x, weight, bn_gamma, bn_beta, bn_mean, bn_var, out_0, out_1):
@@ -177,10 +178,14 @@ def tile_modelnew_kernel(tc, x, weight, bn_gamma, bn_beta, bn_mean, bn_var, out_
         w_load(3)
 
         stat = consts.tile([P, 32], F32, name="stat")
-        o_sb = []
+        o_sb = {}
         for m in range(8):
-            o = outp.tile([P, N], F32, name="o%d" % m)
-            o_sb.append(o)
+            for s in range(N // SW):
+                o_sb[(m, s)] = outp.tile([P, SW], F32, name="o%d_%d" % (m, s))
+
+        def o_view(m, c):
+            lo = CW * c % SW
+            return o_sb[(m, CW * c // SW)][:, lo:lo + CW]
         g_sb = {}
 
         def mx(acc, c, h, j, p):
@@ -194,13 +199,24 @@ def tile_modelnew_kernel(tc, x, weight, bn_gamma, bn_beta, bn_mean, bn_var, out_
                 stop=(p == PASSES - 1),
             )
 
+        pair_sb = {}
+
         def gelu(acc, c, h, j):
             nt = 4 * c + j
-            gt = gtp.tile([P, HW], F32, name="gt", tag="gt")
+            if 2 * c + h < LATE:
+                gt = gtp.tile([P, HW], F32, name="gt", tag="gt")
+                g_sb[(c, h, j)] = gt[:]
+            else:
+                if j % 2 == 0:
+                    gp = ld.tile([P, 2, HW], F32, name="gp", tag="ld")
+                    pair_sb[(c, h)] = gp
+                g_sb[(c, h, j)] = pair_sb[(c, h)][:, j % 2, :]
             nc.scalar.activation(
-                out=gt[:], in_=acc[:], func=ACT.Gelu_apprx_tanh, bias=cc[:, nt:nt + 1], scale=aa[:, nt:nt + 1]
+                out=g_sb[(c, h, j)], in_=acc[:], func=ACT.Gelu_apprx_tanh, bias=cc[:, nt:nt + 1], scale=aa[:, nt:nt + 1]
             )
-            g_sb[(c, h, j)] = gt
+            if 2 * c + h >= LATE:
+                k = 8 * c + 4 * h + j
+                nc.vector.tensor_reduce(out=stat[:, k:k + 1], in_=g_sb[(c, h, j)], axis=AX.X, op=ALU.max)
 
         def back(c, h):
             for mi in range(4):
@@ -212,15 +228,14 @@ def tile_modelnew_kernel(tc, x, weight, bn_gamma, bn_beta, bn_mean, bn_var, out_
                     )
                 k = 8 * c + m
                 nc.vector.tensor_scalar(
-                    out=o_sb[m][:, CW * c:CW * (c + 1)], in0=tp[:], scalar1=0.0, scalar2=None,
+                    out=o_view(m, c), in0=tp[:], scalar1=0.0, scalar2=None,
                     op0=ALU.max, op1=ALU.max, accum_out=stat[:, k:k + 1],
                 )
-                nc.sync.dma_start(out=out_0[P * m:P * (m + 1), CW * c:CW * (c + 1)], in_=o_sb[m][:, CW * c:CW * (c + 1)])
+                nc.sync.dma_start(out=out_0[P * m:P * (m + 1), CW * c:CW * (c + 1)], in_=o_view(m, c))
 
         plan = {0: ((1, 0), (1, 1)), 1: ((1, 2), (1, 3)), 2: ((2, 0), (2, 1)), 3: ((2, 2), (2, 3)),
                 4: ((3, 0), (3, 1)), 5: ((3, 2), (3, 3))}
         units = [(c, h) for c in range(CHUNKS) for h in range(HALVES)]
-        last = len(units) - 1
         for ui, (c, h) in enumerate(units):
             todo = plan.get(ui, ())
             if ui == 0:
@@ -248,27 +263,32 @@ def tile_modelnew_kernel(tc, x, weight, bn_gamma, bn_beta, bn_mean, bn_var, out_
                 if j == 0 and todo:
                     w_weave(todo[0][0], todo[0][1])
                 gelu(acc, c, h, j)
-                if ui == last:
-                    k = 8 * c + 4 * h + j
-                    nc.vector.tensor_reduce(out=stat[:, k:k + 1], in_=g_sb[(c, h, j)][:], axis=AX.X, op=ALU.max)
                 if j == 1 and todo:
                     w_quant(todo[0][0], todo[0][1])
                     w_weave(todo[1][0], todo[1][1])
-                if j == after:
+                if j == after and ui - 1 < LATE:
                     back(units[ui - 1][0], units[ui - 1][1])
                 if j == 2 and todo:
                     w_quant(todo[1][0], todo[1][1])
 
-        c, h = units[last]
-        tps = []
-        for mi in range(4):
-            tp = psum.tile([P, CW], F32, name="tp", tag="tp")
-            tps.append(tp)
-        for j in range(4):
+        def late_turn(c, h):
+            tps = []
             for mi in range(4):
-                nc.tensor.transpose(
-                    out=tps[mi][:, P * j:P * (j + 1)], in_=g_sb[(c, h, j)][:, P * mi:P * (mi + 1)], identity=ident[:]
-                )
+                tp = psum.tile([P, CW], F32, name="tp", tag="tp")
+                for j in range(4):
+                    nc.tensor.transpose(
+                        out=tp[:, P * j:P * (j + 1)], in_=g_sb[(c, h, j)][:, P * mi:P * (mi + 1)], identity=ident[:]
+                    )
+                tps.append(tp)
+            return tps
+
+        def late_empty(c, h, tps):
+            for mi in range(4):
+                m = 4 * h + mi
+                nc.scalar.activation(out=o_view(m, c), in_=tps[mi][:], func=ACT.Relu)
+                nc.sync.dma_start(out=out_0[P * m:P * (m + 1), CW * c:CW * (c + 1)], in_=o_view(m, c))
+
+        first_tps = late_turn(2, 0)
 
         junk = consts.tile([P, 32], F32, name="junk")
         part = consts.tile([P, 1], F32, name="part")
@@ -282,35 +302,34 @@ def tile_modelnew_kernel(tc, x, weight, bn_gamma, bn_beta, bn_mean, bn_var, out_
         inv = consts.tile([P, 1], F32, name="inv")
         nc.vector.reciprocal(out=inv[:], in_=s_all[:])
 
-        for mi in range(4):
-            m = 4 * h + mi
-            nc.scalar.activation(out=o_sb[m][:, CW * c:CW * (c + 1)], in_=tps[mi][:], func=ACT.Relu)
-            nc.sync.dma_start(out=out_0[P * m:P * (m + 1), CW * c:CW * (c + 1)], in_=o_sb[m][:, CW * c:CW * (c + 1)])
+        late_empty(2, 0, first_tps)
+        for c, h in ((3, 0), (2, 1), (3, 1)):
+            late_empty(c, h, late_turn(c, h))
 
-        steps = [(m, s) for m in range(8) for s in range(N // SW)]
-        f8_sb = {}
+        steps = [(m, s) for s in range(N // SW) for m in range(8)]
         tmp_sb = {}
 
         def scale(m, s):
             tmp = ld.tile([P, SW], F32, name="tmp", tag="ld")
-            lo = SW * s
+            sv = SV[s]
             nc.vector.tensor_scalar(
-                out=tmp[:, 0:SV], in0=o_sb[m][:, lo:lo + SV], scalar1=inv[:, 0:1], scalar2=None, op0=ALU.mult
+                out=tmp[:, 0:sv], in0=o_sb[(m, s)][:, 0:sv], scalar1=inv[:, 0:1], scalar2=None, op0=ALU.mult
             )
-            nc.scalar.activation(out=tmp[:, SV:SW], in_=o_sb[m][:, lo + SV:lo + SW], func=ACT.Copy, scale=inv[:, 0:1])
+            if sv < SW:
+                nc.scalar.activation(
+                    out=tmp[:, sv:SW], in_=o_sb[(m, s)][:, sv:SW], func=ACT.Copy, scale=inv[:, 0:1]
+                )
             tmp_sb[(m, s)] = tmp
 
         def cast(m, s):
-            if s == 0:
-                f8 = f8p.tile([P, N], FP8, name="f8", tag="f8")
-                f8_sb[m] = f8
-            f8 = f8_sb[m]
+            f8 = f8p.tile([P, SW], FP8, name="f8", tag="f8")
             tmp = tmp_sb[(m, s)]
             lo = SW * s
-            nc.vector.tensor_copy(out=f8[:, lo:lo + SV], in_=tmp[:, 0:SV], saturate=False)
-            nc.scalar.copy(out=f8[:, lo + SV:lo + SW], in_=tmp[:, SV:SW], saturate=False)
-            if s == N // SW - 1:
-                nc.sync.dma_start(out=out_1[P * m:P * (m + 1), :], in_=f8[:].bitcast(U8))
+            sv = SV[s]
+            nc.vector.tensor_copy(out=f8[:, 0:sv], in_=tmp[:, 0:sv], saturate=False)
+            if sv < SW:
+                nc.scalar.copy(out=f8[:, sv:SW], in_=tmp[:, sv:SW], saturate=False)
+            nc.sync.dma_start(out=out_1[P * m:P * (m + 1), lo:lo + SW], in_=f8[:].bitcast(U8))
 
         scale(steps[0][0], steps[0][1])
         for i in range(1, len(steps)):

@@ -26,6 +26,7 @@ HW = 512
 VW = 288
 SW = 1024
 SV = (1024, 608)
+STATS = 33
 LATE = 4
 
 
@@ -33,7 +34,7 @@ def tile_modelnew_kernel(tc, x, weight, bn_gamma, bn_beta, bn_mean, bn_var, out_
     nc = tc.nc
     with ExitStack() as ctx:
         consts = ctx.enter_context(tc.tile_pool(name="consts", bufs=1))
-        ld = ctx.enter_context(tc.tile_pool(name="ld", bufs=12))
+        ld = ctx.enter_context(tc.tile_pool(name="ld", bufs=14))
         gxp = ctx.enter_context(tc.tile_pool(name="gxp", bufs=4))
         xq = ctx.enter_context(tc.tile_pool(name="xq", bufs=1))
         wgp = ctx.enter_context(tc.tile_pool(name="wgp", bufs=3))
@@ -177,7 +178,7 @@ def tile_modelnew_kernel(tc, x, weight, bn_gamma, bn_beta, bn_mean, bn_var, out_
         w_quant(0, 3)
         w_load(3)
 
-        stat = consts.tile([P, 32], F32, name="stat")
+        stat = consts.tile([P, STATS], F32, name="stat")
         o_sb = {}
         for m in range(8):
             for s in range(N // SW):
@@ -188,20 +189,20 @@ def tile_modelnew_kernel(tc, x, weight, bn_gamma, bn_beta, bn_mean, bn_var, out_
             return o_sb[(m, CW * c // SW)][:, lo:lo + CW]
         g_sb = {}
 
-        def mx(acc, c, h, j, p):
+        def mx(acc, c, h, j, p, lo=0, hi=HW):
             nc.tensor.matmul_mx(
                 out=acc[:],
                 lhsT=wc[(c, p)][:, P * j:P * (j + 1)].bitcast(FP8X4),
                 lhsT_scale=ws[(c, p)][:, P * j:P * (j + 1)],
-                rhs=xc[(p, h)][:].bitcast(FP8X4),
-                rhs_scale=xs[(p, h)][:],
+                rhs=xc[(p, h)][:, lo:hi].bitcast(FP8X4),
+                rhs_scale=xs[(p, h)][:, lo:hi],
                 start=(p == 0),
                 stop=(p == PASSES - 1),
             )
 
         pair_sb = {}
 
-        def gelu(acc, c, h, j):
+        def gelu(acc, c, h, j, lo=0, hi=HW, k=None):
             nt = 4 * c + j
             if 2 * c + h < LATE:
                 gt = gtp.tile([P, HW], F32, name="gt", tag="gt")
@@ -212,11 +213,13 @@ def tile_modelnew_kernel(tc, x, weight, bn_gamma, bn_beta, bn_mean, bn_var, out_
                     pair_sb[(c, h)] = gp
                 g_sb[(c, h, j)] = pair_sb[(c, h)][:, j % 2, :]
             nc.scalar.activation(
-                out=g_sb[(c, h, j)], in_=acc[:], func=ACT.Gelu_apprx_tanh, bias=cc[:, nt:nt + 1], scale=aa[:, nt:nt + 1]
+                out=g_sb[(c, h, j)][:, lo:hi], in_=acc[:], func=ACT.Gelu_apprx_tanh,
+                bias=cc[:, nt:nt + 1], scale=aa[:, nt:nt + 1],
             )
             if 2 * c + h >= LATE:
-                k = 8 * c + 4 * h + j
-                nc.vector.tensor_reduce(out=stat[:, k:k + 1], in_=g_sb[(c, h, j)], axis=AX.X, op=ALU.max)
+                if k is None:
+                    k = 8 * c + 4 * h + j
+                nc.vector.tensor_reduce(out=stat[:, k:k + 1], in_=g_sb[(c, h, j)][:, lo:hi], axis=AX.X, op=ALU.max)
 
         def back(c, h):
             for mi in range(4):
@@ -257,6 +260,13 @@ def tile_modelnew_kernel(tc, x, weight, bn_gamma, bn_beta, bn_mean, bn_var, out_
                 continue
             after = 2 if ui == 1 else 1
             for j in range(4):
+                if ui == len(units) - 1 and j == 3:
+                    for half in range(2):
+                        acc = psum.tile([P, HW // 2], F32, name="acc", tag="acc")
+                        for p in range(PASSES):
+                            mx(acc, c, h, j, p, 256 * half, 256 * (half + 1))
+                        gelu(acc, c, h, j, 256 * half, 256 * (half + 1), 31 + half)
+                    continue
                 acc = psum.tile([P, HW], F32, name="acc", tag="acc")
                 for p in range(PASSES):
                     mx(acc, c, h, j, p)
@@ -271,26 +281,26 @@ def tile_modelnew_kernel(tc, x, weight, bn_gamma, bn_beta, bn_mean, bn_var, out_
                 if j == 2 and todo:
                     w_quant(todo[1][0], todo[1][1])
 
-        def late_turn(c, h):
+        def late_turn(m):
             tps = []
-            for mi in range(4):
+            for c in range(LATE // HALVES, CHUNKS):
                 tp = psum.tile([P, CW], F32, name="tp", tag="tp")
                 for j in range(4):
                     nc.tensor.transpose(
-                        out=tp[:, P * j:P * (j + 1)], in_=g_sb[(c, h, j)][:, P * mi:P * (mi + 1)], identity=ident[:]
+                        out=tp[:, P * j:P * (j + 1)], in_=g_sb[(c, m // 4, j)][:, P * (m % 4):P * (m % 4 + 1)],
+                        identity=ident[:],
                     )
                 tps.append(tp)
             return tps
 
-        def late_empty(c, h, tps):
-            for mi in range(4):
-                m = 4 * h + mi
-                nc.scalar.activation(out=o_view(m, c), in_=tps[mi][:], func=ACT.Relu)
-                nc.sync.dma_start(out=out_0[P * m:P * (m + 1), CW * c:CW * (c + 1)], in_=o_view(m, c))
+        def late_empty(m, tps):
+            for i, c in enumerate(range(LATE // HALVES, CHUNKS)):
+                nc.scalar.activation(out=o_view(m, c), in_=tps[i][:], func=ACT.Relu)
+            nc.sync.dma_start(out=out_0[P * m:P * (m + 1), SW:N], in_=o_sb[(m, 1)][:])
 
-        first_tps = late_turn(2, 0)
+        early = [late_turn(0), late_turn(1)]
 
-        junk = consts.tile([P, 32], F32, name="junk")
+        junk = consts.tile([P, STATS], F32, name="junk")
         part = consts.tile([P, 1], F32, name="part")
         nc.vector.tensor_scalar(
             out=junk[:], in0=stat[:], scalar1=1.0 / 448.0, scalar2=None, op0=ALU.mult, op1=ALU.max, accum_out=part[:]
@@ -302,9 +312,10 @@ def tile_modelnew_kernel(tc, x, weight, bn_gamma, bn_beta, bn_mean, bn_var, out_
         inv = consts.tile([P, 1], F32, name="inv")
         nc.vector.reciprocal(out=inv[:], in_=s_all[:])
 
-        late_empty(2, 0, first_tps)
-        for c, h in ((3, 0), (2, 1), (3, 1)):
-            late_empty(c, h, late_turn(c, h))
+        late_empty(0, early[0])
+        late_empty(1, early[1])
+        for m in range(2, 8):
+            late_empty(m, late_turn(m))
 
         steps = [(m, s) for s in range(N // SW) for m in range(8)]
         tmp_sb = {}

@@ -24,10 +24,11 @@ HALVES = 2
 CW = 512
 HW = 512
 VW = 288
-SW = 1024
-SV = (1024, 608)
 STATS = 33
-LATE = 4
+LATE = 6
+TURNS_FIRST = 2
+S_ROWS = (6, 7)
+CAST_ORDER = (0, 1, 2, 3, 4, 5, 6, 7)
 
 
 def tile_modelnew_kernel(tc, x, weight, bn_gamma, bn_beta, bn_mean, bn_var, out_0, out_1):
@@ -55,6 +56,8 @@ def tile_modelnew_kernel(tc, x, weight, bn_gamma, bn_beta, bn_mean, bn_var, out_
 
         one = consts.tile([P, 1], F32, name="one")
         nc.vector.memset(one[:], 1.0)
+        zero = consts.tile([P, 1], F32, name="zero")
+        nc.vector.memset(zero[:], 0.0)
         warm = consts.tile([P, 1], F32, name="warm")
         nc.scalar.activation(out=warm[:], in_=one[:], func=ACT.Sqrt)
 
@@ -179,14 +182,13 @@ def tile_modelnew_kernel(tc, x, weight, bn_gamma, bn_beta, bn_mean, bn_var, out_
         w_load(3)
 
         stat = consts.tile([P, STATS], F32, name="stat")
-        o_sb = {}
+        o_row = []
         for m in range(8):
-            for s in range(N // SW):
-                o_sb[(m, s)] = outp.tile([P, SW], F32, name="o%d_%d" % (m, s))
+            o_t = outp.tile([P, N], F32, name="o%d" % m)
+            o_row.append(o_t)
 
         def o_view(m, c):
-            lo = CW * c % SW
-            return o_sb[(m, CW * c // SW)][:, lo:lo + CW]
+            return o_row[m][:, CW * c:CW * (c + 1)]
         g_sb = {}
 
         def mx(acc, c, h, j, p, lo=0, hi=HW):
@@ -281,9 +283,12 @@ def tile_modelnew_kernel(tc, x, weight, bn_gamma, bn_beta, bn_mean, bn_var, out_
                 if j == 2 and todo:
                     w_quant(todo[1][0], todo[1][1])
 
+        def late_chunks(m):
+            return [c for (c, h) in units[LATE:] if h == m // 4]
+
         def late_turn(m):
             tps = []
-            for c in range(LATE // HALVES, CHUNKS):
+            for c in late_chunks(m):
                 tp = psum.tile([P, CW], F32, name="tp", tag="tp")
                 for j in range(4):
                     nc.tensor.transpose(
@@ -294,11 +299,13 @@ def tile_modelnew_kernel(tc, x, weight, bn_gamma, bn_beta, bn_mean, bn_var, out_
             return tps
 
         def late_empty(m, tps):
-            for i, c in enumerate(range(LATE // HALVES, CHUNKS)):
+            cs = late_chunks(m)
+            for i, c in enumerate(cs):
                 nc.scalar.activation(out=o_view(m, c), in_=tps[i][:], func=ACT.Relu)
-            nc.sync.dma_start(out=out_0[P * m:P * (m + 1), SW:N], in_=o_sb[(m, 1)][:])
+            nc.sync.dma_start(out=out_0[P * m:P * (m + 1), CW * cs[0]:N], in_=o_row[m][:, CW * cs[0]:N])
 
-        early = [late_turn(0), late_turn(1)]
+        late_rows = [m for m in range(8) if late_chunks(m)]
+        early = [late_turn(m) for m in late_rows[0:TURNS_FIRST]]
 
         junk = consts.tile([P, STATS], F32, name="junk")
         part = consts.tile([P, 1], F32, name="part")
@@ -312,38 +319,22 @@ def tile_modelnew_kernel(tc, x, weight, bn_gamma, bn_beta, bn_mean, bn_var, out_
         inv = consts.tile([P, 1], F32, name="inv")
         nc.vector.reciprocal(out=inv[:], in_=s_all[:])
 
-        late_empty(0, early[0])
-        late_empty(1, early[1])
-        for m in range(2, 8):
-            late_empty(m, late_turn(m))
+        for i, m in enumerate(late_rows):
+            late_empty(m, early[i] if i < TURNS_FIRST else late_turn(m))
 
-        steps = [(m, s) for s in range(N // SW) for m in range(8)]
-        tmp_sb = {}
-
-        def scale(m, s):
-            tmp = ld.tile([P, SW], F32, name="tmp", tag="ld")
-            sv = SV[s]
-            nc.vector.tensor_scalar(
-                out=tmp[:, 0:sv], in0=o_sb[(m, s)][:, 0:sv], scalar1=inv[:, 0:1], scalar2=None, op0=ALU.mult
-            )
-            if sv < SW:
-                nc.scalar.activation(
-                    out=tmp[:, sv:SW], in_=o_sb[(m, s)][:, sv:SW], func=ACT.Copy, scale=inv[:, 0:1]
+        def cast(m):
+            f8 = f8p.tile([P, N], FP8, name="f8", tag="f8")
+            if m in S_ROWS:
+                for lo in range(0, N, 1024):
+                    nc.scalar.activation(
+                        out=f8[:, lo:lo + 1024], in_=o_row[m][:, lo:lo + 1024], func=ACT.Identity,
+                        scale=inv[:, 0:1], bias=zero[:, 0:1], saturate=False,
+                    )
+            else:
+                nc.vector.tensor_scalar(
+                    out=f8[:], in0=o_row[m][:], scalar1=inv[:, 0:1], scalar2=None, op0=ALU.mult, saturate=False,
                 )
-            tmp_sb[(m, s)] = tmp
+            nc.sync.dma_start(out=out_1[P * m:P * (m + 1), :], in_=f8[:].bitcast(U8))
 
-        def cast(m, s):
-            f8 = f8p.tile([P, SW], FP8, name="f8", tag="f8")
-            tmp = tmp_sb[(m, s)]
-            lo = SW * s
-            sv = SV[s]
-            nc.vector.tensor_copy(out=f8[:, 0:sv], in_=tmp[:, 0:sv], saturate=False)
-            if sv < SW:
-                nc.scalar.copy(out=f8[:, sv:SW], in_=tmp[:, sv:SW], saturate=False)
-            nc.sync.dma_start(out=out_1[P * m:P * (m + 1), lo:lo + SW], in_=f8[:].bitcast(U8))
-
-        scale(steps[0][0], steps[0][1])
-        for i in range(1, len(steps)):
-            scale(steps[i][0], steps[i][1])
-            cast(steps[i - 1][0], steps[i - 1][1])
-        cast(steps[-1][0], steps[-1][1])
+        for m in CAST_ORDER:
+            cast(m)

@@ -48,24 +48,25 @@ def tile_modelnew_kernel(tc, x, weight, bn_gamma, bn_beta, bn_mean, bn_var, out_
 
         ident = consts.tile([P, P], F32, name="ident")
         make_identity(nc, ident[:])
-
-        bn_raw = consts.tile([P, P], BF16, name="bn_raw")
-        nc.vector.memset(bn_raw[64:128, :], 0.0)
-        for v, vec in enumerate((bn_gamma, bn_beta, bn_mean, bn_var)):
-            nc.sync.dma_start(out=bn_raw[16 * v:16 * v + 16, :], in_=vec.rearrange("(t p) -> t p", p=P))
-
         one = consts.tile([P, 1], F32, name="one")
         nc.vector.memset(one[:], 1.0)
         zero = consts.tile([P, 1], F32, name="zero")
         nc.vector.memset(zero[:], 0.0)
+        mhalf = consts.tile([P, 16], F32, name="mhalf")
+        nc.gpsimd.memset(mhalf[:], -0.5)
         warm = consts.tile([P, 1], F32, name="warm")
-        nc.scalar.activation(out=warm[:], in_=one[:], func=ACT.Sqrt)
+        nc.scalar.activation(out=warm[:], in_=one[:], func=ACT.Gelu_apprx_tanh)
 
+        bn_raw = consts.tile([P, P], BF16, name="bn_raw")
+        nc.vector.memset(bn_raw[64:128, :], 0.0)
         x_sb = []
         for m in range(8):
             t = ld.tile([P, K], BF16, name="x%d" % m, tag="ld")
             nc.sync.dma_start(out=t[:], in_=x[P * m:P * (m + 1), :])
             x_sb.append(t)
+            if m == 1:
+                for v, vec in enumerate((bn_gamma, bn_beta, bn_mean, bn_var)):
+                    nc.sync.dma_start(out=bn_raw[16 * v:16 * v + 16, :], in_=vec.rearrange("(t p) -> t p", p=P))
         w_raw = {}
 
         def w_load(c):
@@ -79,26 +80,24 @@ def tile_modelnew_kernel(tc, x, weight, bn_gamma, bn_beta, bn_mean, bn_var, out_
 
         w_load(0)
 
-        bn_f = consts.tile([P, P], F32, name="bn_f")
-        nc.vector.tensor_copy(out=bn_f[:], in_=bn_raw[:])
-        bn_ps = psum.tile([P, P], F32, name="bn_ps", tag="tp")
-        nc.tensor.transpose(out=bn_ps[:], in_=bn_f[:], identity=ident[:])
-        bnT = consts.tile([P, 64], F32, name="bnT")
-        nc.vector.tensor_copy(out=bnT[:], in_=bn_ps[:, 0:64])
-        ve = consts.tile([P, 16], F32, name="ve")
-        nc.vector.tensor_scalar(out=ve[:], in0=bnT[:, 48:64], scalar1=EPS, scalar2=None, op0=ALU.add)
-        sd = consts.tile([P, 16], F32, name="sd")
-        nc.scalar.activation(out=sd[:], in_=ve[:], func=ACT.Sqrt)
-        warm2 = consts.tile([P, 1], F32, name="warm2")
-        nc.scalar.activation(out=warm2[:], in_=sd[:, 0:1], func=ACT.Gelu_apprx_tanh)
-        rs = consts.tile([P, 16], F32, name="rs")
-        nc.vector.reciprocal(out=rs[:], in_=sd[:])
         aa = consts.tile([P, 16], F32, name="aa")
-        nc.vector.tensor_tensor(out=aa[:], in0=bnT[:, 0:16], in1=rs[:], op=ALU.mult)
-        ma = consts.tile([P, 16], F32, name="ma")
-        nc.vector.tensor_tensor(out=ma[:], in0=bnT[:, 32:48], in1=aa[:], op=ALU.mult)
         cc = consts.tile([P, 16], F32, name="cc")
-        nc.vector.tensor_tensor(out=cc[:], in0=bnT[:, 16:32], in1=ma[:], op=ALU.subtract)
+
+        def bn_prepare():
+            bn_f = consts.tile([P, P], F32, name="bn_f")
+            nc.vector.tensor_copy(out=bn_f[:], in_=bn_raw[:])
+            bn_ps = psum.tile([P, P], F32, name="bn_ps", tag="tp")
+            nc.tensor.transpose(out=bn_ps[:], in_=bn_f[:], identity=ident[:])
+            bnT = consts.tile([P, 64], F32, name="bnT")
+            nc.vector.tensor_copy(out=bnT[:], in_=bn_ps[:, 0:64])
+            ve = consts.tile([P, 16], F32, name="ve")
+            nc.gpsimd.tensor_scalar(out=ve[:], in0=bnT[:, 48:64], scalar1=EPS, scalar2=None, op0=ALU.add)
+            rs = consts.tile([P, 16], F32, name="rs")
+            nc.gpsimd.tensor_tensor(out=rs[:], in0=ve[:], in1=mhalf[:], op=ALU.pow)
+            nc.gpsimd.tensor_tensor(out=aa[:], in0=bnT[:, 0:16], in1=rs[:], op=ALU.mult)
+            ma = consts.tile([P, 16], F32, name="ma")
+            nc.gpsimd.tensor_tensor(out=ma[:], in0=bnT[:, 32:48], in1=aa[:], op=ALU.mult)
+            nc.gpsimd.tensor_tensor(out=cc[:], in0=bnT[:, 16:32], in1=ma[:], op=ALU.subtract)
 
         xc = {}
         xs = {}
@@ -126,7 +125,7 @@ def tile_modelnew_kernel(tc, x, weight, bn_gamma, bn_beta, bn_mean, bn_var, out_
             gx = gxp.tile([P, 1024], BF16, name="gx", tag="gx", align_bytes=64)
             dst = gx[:].bitcast(F32).rearrange("p (r u) -> p r u", u=2)
             src = xt_ps[(q, g)][:].rearrange("p u r -> p r u")
-            on_scalar = (g >= 2) if q == 0 else (g < 3)
+            on_scalar = g < 3
             if on_scalar:
                 nc.scalar.copy(out=dst, in_=src)
             else:
@@ -162,6 +161,8 @@ def tile_modelnew_kernel(tc, x, weight, bn_gamma, bn_beta, bn_mean, bn_var, out_
             for g in range(PASSES):
                 x_turn(q, g)
                 x_quant(q, g)
+            if q == 0:
+                bn_prepare()
             if q == 1:
                 w_load(1)
         for g in range(PASSES):

@@ -224,8 +224,8 @@ def tile_modelnew_kernel(tc, x, weight, bn_gamma, bn_beta, bn_mean, bn_var, out_
                     k = 8 * c + 4 * h + j
                 nc.vector.tensor_reduce(out=stat[:, k:k + 1], in_=g_sb[(c, h, j)][:, lo:hi], axis=AX.X, op=ALU.max)
 
-        def back(c, h):
-            for mi in range(4):
+        def back(c, h, first, last):
+            for mi in range(first, last):
                 m = 4 * h + mi
                 tp = psum.tile([P, CW], F32, name="tp", tag="tp")
                 for j in range(4):
@@ -280,7 +280,9 @@ def tile_modelnew_kernel(tc, x, weight, bn_gamma, bn_beta, bn_mean, bn_var, out_
                     w_quant(todo[0][0], todo[0][1])
                     w_weave(todo[1][0], todo[1][1])
                 if j == after and ui - 1 < LATE:
-                    back(units[ui - 1][0], units[ui - 1][1])
+                    back(units[ui - 1][0], units[ui - 1][1], 0, 2)
+                if j == after + 1 and ui - 1 < LATE:
+                    back(units[ui - 1][0], units[ui - 1][1], 2, 4)
                 if j == 2 and todo:
                     w_quant(todo[1][0], todo[1][1])
 

@@ -25,7 +25,7 @@ CW = 512
 HW = 512
 VW = 288
 STATS = 33
-LATE = 6
+LATE_UNITS = ((2, 1), (3, 1))
 TURNS_FIRST = 2
 S_ROWS = (6, 7)
 CAST_ORDER = (0, 1, 2, 3, 4, 5, 6, 7)
@@ -207,7 +207,7 @@ def tile_modelnew_kernel(tc, x, weight, bn_gamma, bn_beta, bn_mean, bn_var, out_
 
         def gelu(acc, c, h, j, lo=0, hi=HW, k=None):
             nt = 4 * c + j
-            if 2 * c + h < LATE:
+            if (c, h) not in LATE_UNITS:
                 gt = gtp.tile([P, HW], F32, name="gt", tag="gt")
                 g_sb[(c, h, j)] = gt[:]
             else:
@@ -219,7 +219,7 @@ def tile_modelnew_kernel(tc, x, weight, bn_gamma, bn_beta, bn_mean, bn_var, out_
                 out=g_sb[(c, h, j)][:, lo:hi], in_=acc[:], func=ACT.Gelu_apprx_tanh,
                 bias=cc[:, nt:nt + 1], scale=aa[:, nt:nt + 1],
             )
-            if 2 * c + h >= LATE:
+            if (c, h) in LATE_UNITS:
                 if k is None:
                     k = 8 * c + 4 * h + j
                 nc.vector.tensor_reduce(out=stat[:, k:k + 1], in_=g_sb[(c, h, j)][:, lo:hi], axis=AX.X, op=ALU.max)
@@ -279,15 +279,15 @@ def tile_modelnew_kernel(tc, x, weight, bn_gamma, bn_beta, bn_mean, bn_var, out_
                 if j == 1 and todo:
                     w_quant(todo[0][0], todo[0][1])
                     w_weave(todo[1][0], todo[1][1])
-                if j == after and ui - 1 < LATE:
+                if j == after and units[ui - 1] not in LATE_UNITS:
                     back(units[ui - 1][0], units[ui - 1][1], 0, 2)
-                if j == after + 1 and ui - 1 < LATE:
+                if j == after + 1 and units[ui - 1] not in LATE_UNITS:
                     back(units[ui - 1][0], units[ui - 1][1], 2, 4)
                 if j == 2 and todo:
                     w_quant(todo[1][0], todo[1][1])
 
         def late_chunks(m):
-            return [c for (c, h) in units[LATE:] if h == m // 4]
+            return [c for (c, h) in LATE_UNITS if h == m // 4]
 
         def late_turn(m):
             tps = []

@@ -23,12 +23,13 @@ CHUNKS = 4
 HALVES = 2
 CW = 512
 HW = 512
-VW = 288
+VW = (256, 400, 288, 288)
 STATS = 33
 LATE_UNITS = ((2, 1), (3, 1))
 TURNS_FIRST = 2
 S_ROWS = (6, 7)
 CAST_ORDER = (0, 1, 2, 3, 4, 5, 6, 7)
+BACK_IN = {2: 0, 3: 1, 4: 2, 5: 3, 6: 4, 7: 6}
 
 
 def tile_modelnew_kernel(tc, x, weight, bn_gamma, bn_beta, bn_mean, bn_var, out_0, out_1):
@@ -39,8 +40,8 @@ def tile_modelnew_kernel(tc, x, weight, bn_gamma, bn_beta, bn_mean, bn_var, out_
         gxp = ctx.enter_context(tc.tile_pool(name="gxp", bufs=4))
         xq = ctx.enter_context(tc.tile_pool(name="xq", bufs=1))
         wgp = ctx.enter_context(tc.tile_pool(name="wgp", bufs=3))
-        wq = ctx.enter_context(tc.tile_pool(name="wq", bufs=1))
-        gtp = ctx.enter_context(tc.tile_pool(name="gtp", bufs=8))
+        wq = ctx.enter_context(tc.tile_pool(name="wq", bufs=2))
+        gtp = ctx.enter_context(tc.tile_pool(name="gtp", bufs=12))
         outp = ctx.enter_context(tc.tile_pool(name="outp", bufs=1))
         f8p = ctx.enter_context(tc.tile_pool(name="f8p", bufs=8))
         psum = ctx.enter_context(tc.psum_pool(name="psum", bufs=4))
@@ -139,19 +140,20 @@ def tile_modelnew_kernel(tc, x, weight, bn_gamma, bn_beta, bn_mean, bn_var, out_
         def w_weave(c, p):
             wr = w_raw[(c, p)]
             wg = wgp.tile([P, CW, 4], BF16, name="wg", tag="wg", align_bytes=64)
+            vw = VW[c]
             nc.vector.tensor_copy(
-                out=wg[:, 0:VW, :].rearrange("p (c i) j -> p c j i", i=4),
-                in_=wr[:, :, 0:VW].rearrange("p j (c i) -> p c j i", i=4),
+                out=wg[:, 0:vw, :].rearrange("p (c i) j -> p c j i", i=4),
+                in_=wr[:, :, 0:vw].rearrange("p j (c i) -> p c j i", i=4),
             )
             nc.scalar.copy(
-                out=wg[:, VW:CW, :].rearrange("p (c i) j -> p c j i", i=4),
-                in_=wr[:, :, VW:CW].rearrange("p j (c i) -> p c j i", i=4),
+                out=wg[:, vw:CW, :].rearrange("p (c i) j -> p c j i", i=4),
+                in_=wr[:, :, vw:CW].rearrange("p j (c i) -> p c j i", i=4),
             )
             wg_sb[(c, p)] = wg
 
         def w_quant(c, p):
-            wc[(c, p)] = wq.tile([P, CW], U32, name="wc%d_%d" % (c, p), align_bytes=64)
-            ws[(c, p)] = wq.tile([P, CW], U8, name="ws%d_%d" % (c, p), align_bytes=64)
+            wc[(c, p)] = wq.tile([P, CW], U32, name="wc%d" % p, tag="wc%d" % p, align_bytes=64)
+            ws[(c, p)] = wq.tile([P, CW], U8, name="ws%d" % p, tag="ws%d" % p, align_bytes=64)
             nc.vector.quantize_mx(
                 out=wc[(c, p)][:].bitcast(FP8X4), scales=ws[(c, p)][:],
                 in_=wg_sb[(c, p)][:].rearrange("p w j -> p (w j)"),
@@ -261,7 +263,8 @@ def tile_modelnew_kernel(tc, x, weight, bn_gamma, bn_beta, bn_mean, bn_var, out_
                 gelu(accs[3], c, h, 3)
                 w_quant(1, 1)
                 continue
-            after = 2 if ui == 1 else 1
+            after = 1
+            goes_back = BACK_IN.get(ui)
             for j in range(4):
                 if ui == len(units) - 1 and j == 3:
                     for half in range(2):
@@ -279,10 +282,10 @@ def tile_modelnew_kernel(tc, x, weight, bn_gamma, bn_beta, bn_mean, bn_var, out_
                 if j == 1 and todo:
                     w_quant(todo[0][0], todo[0][1])
                     w_weave(todo[1][0], todo[1][1])
-                if j == after and units[ui - 1] not in LATE_UNITS:
-                    back(units[ui - 1][0], units[ui - 1][1], 0, 2)
-                if j == after + 1 and units[ui - 1] not in LATE_UNITS:
-                    back(units[ui - 1][0], units[ui - 1][1], 2, 4)
+                if j == after and goes_back is not None:
+                    back(units[goes_back][0], units[goes_back][1], 0, 2)
+                if j == after + 1 and goes_back is not None:
+                    back(units[goes_back][0], units[goes_back][1], 2, 4)
                 if j == 2 and todo:
                     w_quant(todo[1][0], todo[1][1])
 

@@ -23,7 +23,7 @@ CHUNKS = 4
 HALVES = 2
 CW = 512
 HW = 512
-VW = (256, 400, 288, 288)
+VW = (224, 320, 288, 288)
 STATS = 33
 LATE_UNITS = ((2, 1), (3, 1))
 TURNS_FIRST = 2
@@ -248,20 +248,32 @@ def tile_modelnew_kernel(tc, x, weight, bn_gamma, bn_beta, bn_mean, bn_var, out_
             todo = plan.get(ui, ())
             if ui == 0:
                 accs = []
-                for j in range(4):
-                    acc = psum.tile([P, HW], F32, name="acc", tag="acc")
-                    accs.append(acc)
-                for p in range(PASSES):
+                for hh in range(HALVES):
                     for j in range(4):
-                        mx(accs[j], c, h, j, p)
+                        acc = psum.tile([P, HW], F32, name="acc", tag=("acc" if hh == 0 else "tp"))
+                        accs.append(acc)
+                for p in range(PASSES):
+                    for hh in range(HALVES):
+                        for j in range(4):
+                            mx(accs[4 * hh + j], 0, hh, j, p)
                 w_weave(1, 0)
-                gelu(accs[0], c, h, 0)
-                gelu(accs[1], c, h, 1)
+                gelu(accs[0], 0, 0, 0)
+                gelu(accs[1], 0, 0, 1)
                 w_weave(1, 1)
                 w_quant(1, 0)
-                gelu(accs[2], c, h, 2)
-                gelu(accs[3], c, h, 3)
+                gelu(accs[2], 0, 0, 2)
+                gelu(accs[3], 0, 0, 3)
                 w_quant(1, 1)
+                w_weave(1, 2)
+                gelu(accs[4], 0, 1, 0)
+                gelu(accs[5], 0, 1, 1)
+                w_quant(1, 2)
+                w_weave(1, 3)
+                gelu(accs[6], 0, 1, 2)
+                w_quant(1, 3)
+                gelu(accs[7], 0, 1, 3)
+                continue
+            if ui == 1:
                 continue
             after = 1
             goes_back = BACK_IN.get(ui)

@@ -23,7 +23,7 @@ CHUNKS = 4
 HALVES = 2
 CW = 512
 HW = 512
-VW = (224, 320, 288, 288)
+VW = (192, 256, 288, 288)
 STATS = 33
 LATE_UNITS = ((2, 1), (3, 1))
 TURNS_FIRST = 2
@@ -61,6 +61,19 @@ def tile_modelnew_kernel(tc, x, weight, bn_gamma, bn_beta, bn_mean, bn_var, out_
         bn_raw = consts.tile([P, P], BF16, name="bn_raw")
         nc.vector.memset(bn_raw[64:128, :], 0.0)
         x_sb = []
+        w_raw = {}
+
+        def w_load(c, first=0):
+            for p in range(first, PASSES):
+                t = ld.tile([P, 4, CW], BF16, name="w%d_%d" % (c, p), tag="ld")
+                nc.sync.dma_start(
+                    out=t[:],
+                    in_=weight[512 * p:512 * (p + 1), CW * c:CW * (c + 1)].rearrange("(p j) w -> p j w", j=4),
+                )
+                w_raw[(c, p)] = t
+                if first == 0 and c == 0:
+                    return
+
         for m in range(8):
             t = ld.tile([P, K], BF16, name="x%d" % m, tag="ld")
             nc.sync.dma_start(out=t[:], in_=x[P * m:P * (m + 1), :])
@@ -68,18 +81,9 @@ def tile_modelnew_kernel(tc, x, weight, bn_gamma, bn_beta, bn_mean, bn_var, out_
             if m == 1:
                 for v, vec in enumerate((bn_gamma, bn_beta, bn_mean, bn_var)):
                     nc.sync.dma_start(out=bn_raw[16 * v:16 * v + 16, :], in_=vec.rearrange("(t p) -> t p", p=P))
-        w_raw = {}
-
-        def w_load(c):
-            for p in range(PASSES):
-                t = ld.tile([P, 4, CW], BF16, name="w%d_%d" % (c, p), tag="ld")
-                nc.sync.dma_start(
-                    out=t[:],
-                    in_=weight[512 * p:512 * (p + 1), CW * c:CW * (c + 1)].rearrange("(p j) w -> p j w", j=4),
-                )
-                w_raw[(c, p)] = t
-
-        w_load(0)
+            if m == 5:
+                w_load(0)
+        w_load(0, 1)
 
         aa = consts.tile([P, 16], F32, name="aa")
         cc = consts.tile([P, 16], F32, name="cc")

@@ -113,7 +113,7 @@ def tile_modelnew_kernel(tc, x, weight, bn_gamma, bn_beta, bn_mean, bn_var, out_
         xt_ps = {}
 
         def x_turn(q, g):
-            xt = psum.tile([P, 2, 256], F32, name="xt", tag="tp")
+            xt = psum.tile([P, 2, 256], F32, name="xt", tag=("acc" if q == 2 else "tp"))
             for mi in range(2):
                 words = x_sb[2 * q + mi][:].bitcast(F32)
                 for u in range(2):

from contextlib import ExitStack

import concourse.mybir as mybir
from concourse.masks import make_identity

B, K, N = 1024, 2048, 2048
EPS = 1e-5
FLOPS = 2 * B * K * N

F32 = mybir.dt.float32
BF16 = mybir.dt.bfloat16
U32 = mybir.dt.uint32
U8 = mybir.dt.uint8
FP8X4 = mybir.dt.float8_e4m3fn_x4
FP8 = mybir.dt.float8_e4m3fn
ACT = mybir.ActivationFunctionType
ALU = mybir.AluOpType
AX = mybir.AxisListType

P = 128
PASSES = 4
CHUNKS = 4
HALVES = 2
CW = 512
HW = 512
VW = (192, 256, 288, 288)
STATS = 33
LATE_UNITS = ((2, 1), (3, 1))
TURNS_FIRST = 2
S_ROWS = (6, 7)
CAST_ORDER = (0, 1, 2, 3, 4, 5, 6, 7)
BACK_IN = {2: 0, 3: 1, 4: 2, 5: 3, 6: 4, 7: 6}


def tile_modelnew_kernel(tc, x, weight, bn_gamma, bn_beta, bn_mean, bn_var, out_0, out_1):
    nc = tc.nc
    with ExitStack() as ctx:
        consts = ctx.enter_context(tc.tile_pool(name="consts", bufs=1))
        ld = ctx.enter_context(tc.tile_pool(name="ld", bufs=14))
        gxp = ctx.enter_context(tc.tile_pool(name="gxp", bufs=4))
        xq = ctx.enter_context(tc.tile_pool(name="xq", bufs=1))
        wgp = ctx.enter_context(tc.tile_pool(name="wgp", bufs=3))
        wq = ctx.enter_context(tc.tile_pool(name="wq", bufs=2))
        gtp = ctx.enter_context(tc.tile_pool(name="gtp", bufs=12))
        outp = ctx.enter_context(tc.tile_pool(name="outp", bufs=1))
        f8p = ctx.enter_context(tc.tile_pool(name="f8p", bufs=8))
        psum = ctx.enter_context(tc.psum_pool(name="psum", bufs=4))
        ctx.enter_context(tc.manual_schedule(engines={mybir.EngineType.PE}))

        ident = consts.tile([P, P], F32, name="ident")
        make_identity(nc, ident[:])
        one = consts.tile([P, 1], F32, name="one")
        nc.vector.memset(one[:], 1.0)
        zero = consts.tile([P, 1], F32, name="zero")
        nc.vector.memset(zero[:], 0.0)
        mhalf = consts.tile([P, 16], F32, name="mhalf")
        nc.gpsimd.memset(mhalf[:], -0.5)
        warm = consts.tile([P, 1], F32, name="warm")
        nc.scalar.activation(out=warm[:], in_=one[:], func=ACT.Gelu_apprx_tanh)

        bn_raw = consts.tile([P, P], BF16, name="bn_raw")
        nc.vector.memset(bn_raw[64:128, :], 0.0)
        x_sb = []
        w_raw = {}

        def w_load(c, first=0):
            for p in range(first, PASSES):
                t = ld.tile([P, 4, CW], BF16, name="w%d_%d" % (c, p), tag="ld")
                nc.sync.dma_start(
                    out=t[:],
                    in_=weight[512 * p:512 * (p + 1), CW * c:CW * (c + 1)].rearrange("(p j) w -> p j w", j=4),
                )
                w_raw[(c, p)] = t
                if first == 0 and c == 0:
                    return

        for m in range(8):
            t = ld.tile([P, K], BF16, name="x%d" % m, tag="ld")
            nc.sync.dma_start(out=t[:], in_=x[P * m:P * (m + 1), :])
            x_sb.append(t)
            if m == 1:
                for v, vec in enumerate((bn_gamma, bn_beta, bn_mean, bn_var)):
                    nc.sync.dma_start(out=bn_raw[16 * v:16 * v + 16, :], in_=vec.rearrange("(t p) -> t p", p=P))
            if m == 5:
                w_load(0)
        w_load(0, 1)

        aa = consts.tile([P, 16], F32, name="aa")
        cc = consts.tile([P, 16], F32, name="cc")

        def bn_prepare():
            bn_f = consts.tile([P, P], F32, name="bn_f")
            nc.vector.tensor_copy(out=bn_f[:], in_=bn_raw[:])
            bn_ps = psum.tile([P, P], F32, name="bn_ps", tag="tp")
            nc.tensor.transpose(out=bn_ps[:], in_=bn_f[:], identity=ident[:])
            bnT = consts.tile([P, 64], F32, name="bnT")
            nc.vector.tensor_copy(out=bnT[:], in_=bn_ps[:, 0:64])
            ve = consts.tile([P, 16], F32, name="ve")
            nc.gpsimd.tensor_scalar(out=ve[:], in0=bnT[:, 48:64], scalar1=EPS, scalar2=None, op0=ALU.add)
            rs = consts.tile([P, 16], F32, name="rs")
            nc.gpsimd.tensor_tensor(out=rs[:], in0=ve[:], in1=mhalf[:], op=ALU.pow)
            nc.gpsimd.tensor_tensor(out=aa[:], in0=bnT[:, 0:16], in1=rs[:], op=ALU.mult)
            ma = consts.tile([P, 16], F32, name="ma")
            nc.gpsimd.tensor_tensor(out=ma[:], in0=bnT[:, 32:48], in1=aa[:], op=ALU.mult)
            nc.gpsimd.tensor_tensor(out=cc[:], in0=bnT[:, 16:32], in1=ma[:], op=ALU.subtract)

        xc = {}
        xs = {}
        for g in range(PASSES):
            for h in range(HALVES):
                xc[(g, h)] = xq.tile([P, HW], U32, name="xc%d_%d" % (g, h), align_bytes=64)
                xs[(g, h)] = xq.tile([P, HW], U8, name="xs%d_%d" % (g, h), align_bytes=64)
        xt_ps = {}

        def x_turn(q, g):
            xt = psum.tile([P, 2, 256], F32, name="xt", tag=("acc" if q == 2 else "tp"))
            for mi in range(2):
                words = x_sb[2 * q + mi][:].bitcast(F32)
                for u in range(2):
                    nc.tensor.transpose(
                        out=xt[:, u, P * mi:P * (mi + 1)],
                        in_=words[:, 256 * g + u:256 * (g + 1):2],
                        identity=ident[:],
                    )
            xt_ps[(q, g)] = xt

        def x_quant(q, g):
            h = q // 2
            cols = slice(256 * (q % 2), 256 * (q % 2) + 256)
            gx = gxp.tile([P, 1024], BF16, name="gx", tag="gx", align_bytes=64)
            dst = gx[:].bitcast(F32).rearrange("p (r u) -> p r u", u=2)
            src = xt_ps[(q, g)][:].rearrange("p u r -> p r u")
            on_scalar = g < 3
            if on_scalar:
                nc.scalar.copy(out=dst, in_=src)
            else:
                nc.vector.tensor_copy(out=dst, in_=src)
            nc.vector.quantize_mx(out=xc[(g, h)][:, cols].bitcast(FP8X4), scales=xs[(g, h)][:, cols], in_=gx[:])

        wc = {}
        ws = {}
        wg_sb = {}

        def w_weave(c, p):
            wr = w_raw[(c, p)]
            wg = wgp.tile([P, CW, 4], BF16, name="wg", tag="wg", align_bytes=64)
            vw = VW[c]
            nc.vector.tensor_copy(
                out=wg[:, 0:vw, :].rearrange("p (c i) j -> p c j i", i=4),
                in_=wr[:, :, 0:vw].rearrange("p j (c i) -> p c j i", i=4),
            )
            nc.scalar.copy(
                out=wg[:, vw:CW, :].rearrange("p (c i) j -> p c j i", i=4),
                in_=wr[:, :, vw:CW].rearrange("p j (c i) -> p c j i", i=4),
            )
            wg_sb[(c, p)] = wg

        def w_quant(c, p):
            wc[(c, p)] = wq.tile([P, CW], U32, name="wc%d" % p, tag="wc%d" % p, align_bytes=64)
            ws[(c, p)] = wq.tile([P, CW], U8, name="ws%d" % p, tag="ws%d" % p, align_bytes=64)
            nc.vector.quantize_mx(
                out=wc[(c, p)][:].bitcast(FP8X4), scales=ws[(c, p)][:],
                in_=wg_sb[(c, p)][:].rearrange("p w j -> p (w j)"),
            )

        for q in range(3):
            for g in range(PASSES):
                x_turn(q, g)
                x_quant(q, g)
            if q == 0:
                bn_prepare()
            if q == 1:
                w_load(1)
        for g in range(PASSES):
            x_turn(3, g)
        w_load(2)
        w_weave(0, 0)
        w_quant(0, 0)
        x_quant(3, 0)
        x_quant(3, 1)
        w_weave(0, 1)
        w_quant(0, 1)
        x_quant(3, 2)
        x_quant(3, 3)
        w_weave(0, 2)
        w_quant(0, 2)
        w_weave(0, 3)
        w_quant(0, 3)
        w_load(3)

        stat = consts.tile([P, STATS], F32, name="stat")
        o_row = []
        for m in range(8):
            o_t = outp.tile([P, N], F32, name="o%d" % m)
            o_row.append(o_t)

        def o_view(m, c):
            return o_row[m][:, CW * c:CW * (c + 1)]
        g_sb = {}

        def mx(acc, c, h, j, p, lo=0, hi=HW):
            nc.tensor.matmul_mx(
                out=acc[:],
                lhsT=wc[(c, p)][:, P * j:P * (j + 1)].bitcast(FP8X4),
                lhsT_scale=ws[(c, p)][:, P * j:P * (j + 1)],
                rhs=xc[(p, h)][:, lo:hi].bitcast(FP8X4),
                rhs_scale=xs[(p, h)][:, lo:hi],
                start=(p == 0),
                stop=(p == PASSES - 1),
            )

        pair_sb = {}

        def gelu(acc, c, h, j, lo=0, hi=HW, k=None):
            nt = 4 * c + j
            if (c, h) not in LATE_UNITS:
                gt = gtp.tile([P, HW], F32, name="gt", tag="gt")
                g_sb[(c, h, j)] = gt[:]
            else:
                if j % 2 == 0:
                    gp = ld.tile([P, 2, HW], F32, name="gp", tag="ld")
                    pair_sb[(c, h)] = gp
                g_sb[(c, h, j)] = pair_sb[(c, h)][:, j % 2, :]
            nc.scalar.activation(
                out=g_sb[(c, h, j)][:, lo:hi], in_=acc[:], func=ACT.Gelu_apprx_tanh,
                bias=cc[:, nt:nt + 1], scale=aa[:, nt:nt + 1],
            )
            if (c, h) in LATE_UNITS:
                if k is None:
                    k = 8 * c + 4 * h + j
                nc.vector.tensor_reduce(out=stat[:, k:k + 1], in_=g_sb[(c, h, j)][:, lo:hi], axis=AX.X, op=ALU.max)

        def back(c, h, first, last):
            for mi in range(first, last):
                m = 4 * h + mi
                tp = psum.tile([P, CW], F32, name="tp", tag="tp")
                for j in range(4):
                    nc.tensor.transpose(
                        out=tp[:, P * j:P * (j + 1)], in_=g_sb[(c, h, j)][:, P * mi:P * (mi + 1)], identity=ident[:]
                    )
                k = 8 * c + m
                nc.vector.tensor_scalar(
                    out=o_view(m, c), in0=tp[:], scalar1=0.0, scalar2=None,
                    op0=ALU.max, op1=ALU.max, accum_out=stat[:, k:k + 1],
                )
                nc.sync.dma_start(out=out_0[P * m:P * (m + 1), CW * c:CW * (c + 1)], in_=o_view(m, c))

        plan = {0: ((1, 0), (1, 1)), 1: ((1, 2), (1, 3)), 2: ((2, 0), (2, 1)), 3: ((2, 2), (2, 3)),
                4: ((3, 0), (3, 1)), 5: ((3, 2), (3, 3))}
        units = [(c, h) for c in range(CHUNKS) for h in range(HALVES)]
        for ui, (c, h) in enumerate(units):
            todo = plan.get(ui, ())
            if ui == 0:
                accs = []
                for hh in range(HALVES):
                    for j in range(4):
                        acc = psum.tile([P, HW], F32, name="acc", tag=("acc" if hh == 0 else "tp"))
                        accs.append(acc)
                for p in range(PASSES):
                    for hh in range(HALVES):
                        for j in range(4):
                            mx(accs[4 * hh + j], 0, hh, j, p)
                w_weave(1, 0)
                gelu(accs[0], 0, 0, 0)
                gelu(accs[1], 0, 0, 1)
                w_weave(1, 1)
                w_quant(1, 0)
                gelu(accs[2], 0, 0, 2)
                gelu(accs[3], 0, 0, 3)
                w_quant(1, 1)
                w_weave(1, 2)
                gelu(accs[4], 0, 1, 0)
                gelu(accs[5], 0, 1, 1)
                w_quant(1, 2)
                w_weave(1, 3)
                gelu(accs[6], 0, 1, 2)
                w_quant(1, 3)
                gelu(accs[7], 0, 1, 3)
                continue
            if ui == 1:
                continue
            after = 1
            goes_back = BACK_IN.get(ui)
            for j in range(4):
                if ui == len(units) - 1 and j == 3:
                    for half in range(2):
                        acc = psum.tile([P, HW // 2], F32, name="acc", tag="acc")
                        for p in range(PASSES):
                            mx(acc, c, h, j, p, 256 * half, 256 * (half + 1))
                        gelu(acc, c, h, j, 256 * half, 256 * (half + 1), 31 + half)
                    continue
                acc = psum.tile([P, HW], F32, name="acc", tag="acc")
                for p in range(PASSES):
                    mx(acc, c, h, j, p)
                if j == 0 and todo:
                    w_weave(todo[0][0], todo[0][1])
                gelu(acc, c, h, j)
                if j == 1 and todo:
                    w_quant(todo[0][0], todo[0][1])
                    w_weave(todo[1][0], todo[1][1])
                if j == after and goes_back is not None:
                    back(units[goes_back][0], units[goes_back][1], 0, 2)
                if j == after + 1 and goes_back is not None:
                    back(units[goes_back][0], units[goes_back][1], 2, 4)
                if j == 2 and todo:
                    w_quant(todo[1][0], todo[1][1])

        def late_chunks(m):
            return [c for (c, h) in LATE_UNITS if h == m // 4]

        def late_turn(m):
            tps = []
            for c in late_chunks(m):
                tp = psum.tile([P, CW], F32, name="tp", tag="tp")
                for j in range(4):
                    nc.tensor.transpose(
                        out=tp[:, P * j:P * (j + 1)], in_=g_sb[(c, m // 4, j)][:, P * (m % 4):P * (m % 4 + 1)],
                        identity=ident[:],
                    )
                tps.append(tp)
            return tps

        def late_empty(m, tps):
            cs = late_chunks(m)
            for i, c in enumerate(cs):
                nc.scalar.activation(out=o_view(m, c), in_=tps[i][:], func=ACT.Relu)
            nc.sync.dma_start(out=out_0[P * m:P * (m + 1), CW * cs[0]:N], in_=o_row[m][:, CW * cs[0]:N])

        late_rows = [m for m in range(8) if late_chunks(m)]
        early = [late_turn(m) for m in late_rows[0:TURNS_FIRST]]

        junk = consts.tile([P, STATS], F32, name="junk")
        part = consts.tile([P, 1], F32, name="part")
        nc.vector.tensor_scalar(
            out=junk[:], in0=stat[:], scalar1=1.0 / 448.0, scalar2=None, op0=ALU.mult, op1=ALU.max, accum_out=part[:]
        )
        pt = psum.tile([P, P], F32, name="pt", tag="acc")
        nc.tensor.transpose(out=pt[:], in_=part[:, 0:1].to_broadcast([P, P]), identity=ident[:])
        s_all = consts.tile([P, 1], F32, name="s_all")
        nc.vector.tensor_reduce(out=s_all[:], in_=pt[:], axis=AX.X, op=ALU.max)
        inv = consts.tile([P, 1], F32, name="inv")
        nc.vector.reciprocal(out=inv[:], in_=s_all[:])

        for i, m in enumerate(late_rows):
            late_empty(m, early[i] if i < TURNS_FIRST else late_turn(m))

        def cast(m):
            f8 = f8p.tile([P, N], FP8, name="f8", tag="f8")
            if m in S_ROWS:
                for lo in range(0, N, 1024):
                    nc.scalar.activation(
                        out=f8[:, lo:lo + 1024], in_=o_row[m][:, lo:lo + 1024], func=ACT.Identity,
                        scale=inv[:, 0:1], bias=zero[:, 0:1], saturate=False,
                    )
            else:
                nc.vector.tensor_scalar(
                    out=f8[:], in0=o_row[m][:], scalar1=inv[:, 0:1], scalar2=None, op0=ALU.mult, saturate=False,
                )
            nc.sync.dma_start(out=out_1[P * m:P * (m + 1), :], in_=f8[:].bitcast(U8))

        for m in CAST_ORDER:
            cast(m)
